import numpy as np
import ml_dtypes


def mxq(x, axis, fmt="e4m3"):
    dtype, down = {"e4m3": (ml_dtypes.float8_e4m3fn, 7), "e5m2": (ml_dtypes.float8_e5m2, 14)}[fmt]
    v = np.moveaxis(np.asarray(x, np.float32).astype(ml_dtypes.bfloat16).astype(np.float64), axis, -1)
    blocks = v.reshape(v.shape[:-1] + (-1, 32))
    amax = np.abs(blocks).max(-1, keepdims=True)
    byte = np.maximum(np.where(amax > 0, np.frexp(amax)[1] - 1 + 127, 0) - down, 1)
    scale = np.exp2(byte - 127.0)
    codes = (blocks / scale).astype(np.float32).astype(dtype).astype(np.float64)
    return np.moveaxis((codes * scale).reshape(v.shape), -1, axis)


WIDE = False


def mx_kscale(k):
    if not WIDE:
        return np.ones(k)
    levels = np.array([10, -10, 5, -5, 0])
    if k % 512:
        return np.exp2(np.random.permutation(np.resize(levels, k // 32))).repeat(32)
    a = np.empty((k // 512, 16))
    for p in range(k // 512):
        a[p, :8] = np.random.permutation(np.resize(levels, 8))
        for g in range(8):
            far = levels[np.abs(levels - a[p, g]) >= 10]
            a[p, g + 8] = far[np.random.randint(len(far))]
    return np.exp2(a.ravel()).repeat(32)


BF16 = ml_dtypes.bfloat16


def bf(x):
    return np.asarray(x, np.float32).astype(BF16)


def f64(x):
    return np.asarray(x).astype(np.float64)


E2M1 = np.array([0.0, 0.5, 1.0, 1.5, 2.0, 3.0, 4.0, 6.0, -0.0, -0.5, -1.0, -1.5, -2.0, -3.0, -4.0, -6.0])


def pack_weight(w, fmt):
    k, n = w.shape
    w = f64(bf(w)).reshape(k // 32, 32, n)
    amax = np.abs(w).max(1)
    if fmt == "e4m3":
        byte = np.frexp(amax)[1] - 1 + 127 - 7
    else:
        mant, ex = np.frexp(amax / 6.0)
        byte = np.where(mant > 0.5, ex, ex - 1) + 127
    byte = np.clip(np.where(amax > 0, byte, 1), 1, 254)
    scaled = (w * np.exp2(127.0 - byte)[:, None, :]).reshape(k, n).astype(np.float32)
    by_word = np.ascontiguousarray(scaled.reshape(k // 512, 128, 4, n).transpose(0, 1, 3, 2))
    if fmt == "e4m3":
        words = by_word.astype(ml_dtypes.float8_e4m3fn).view(np.uint8)
    else:
        c = by_word.astype(ml_dtypes.float4_e2m1fn).view(np.uint8) & 0xF
        words = c[..., 0::2] | (c[..., 1::2] << 4)
    return np.ascontiguousarray(words), np.ascontiguousarray(byte.astype(np.uint8).reshape(k // 512, 16, n))


def unpack_weight(words, scales, fmt):
    g, p, n, _ = words.shape
    if fmt == "e4m3":
        vals = np.ascontiguousarray(words).view(ml_dtypes.float8_e4m3fn).astype(np.float64)
    else:
        nib = np.empty((g, p, n, 4), np.uint8)
        nib[..., 0::2] = words & 0xF
        nib[..., 1::2] = words >> 4
        vals = E2M1[nib]
    vals = vals * np.repeat(np.exp2(scales.astype(np.float64) - 127.0), 8, axis=1)[..., None]
    return vals.transpose(0, 1, 3, 2).reshape(g * 512, n)
def pack4(w):
    words, scales = pack_weight(w, "e2m1")
    return words.reshape(words.shape[0], 128, -1), scales


def unpack4(words, scales):
    return unpack_weight(words.reshape(words.shape[0], 128, -1, 2), scales, "e2m1")


B, S, E, H, W = 32, 32, 512, 8, 16


def draw0():
    s = mx_kscale(E)
    t = mx_kscale(2 * E)
    th, tv = t[:E], t[E:]
    h_ctx = bf(np.random.standard_normal((B, S, E)) * 0.35 * s)
    v_ctx = bf(np.random.standard_normal((B, S, E)) * 0.35 * s)
    h_out_w = np.random.standard_normal((E, E)) * 2.5 / np.sqrt(E) / s[None, :] * th[:, None]
    h_out_b = bf(np.random.standard_normal(E) * 0.2 * th)
    v_out_w = np.random.standard_normal((E, E)) * 2.5 / np.sqrt(E) / s[None, :] * tv[:, None]
    v_out_b = bf(np.random.standard_normal(E) * 0.2 * tv)
    mlp_w1 = np.random.standard_normal((E, 2 * E)) / np.sqrt(2 * E) / t[None, :]
    mlp_b1 = bf(np.random.standard_normal(E) * 0.2)
    h_out_w_words, h_out_w_scales = pack4(h_out_w.T)
    v_out_w_words, v_out_w_scales = pack4(v_out_w.T)
    mlp_w1_words, mlp_w1_scales = pack4(mlp_w1.T)
    return {
        "h_ctx": h_ctx,
        "v_ctx": v_ctx,
        "h_out_w_words": h_out_w_words,
        "h_out_w_scales": h_out_w_scales,
        "h_out_b": h_out_b,
        "v_out_w_words": v_out_w_words,
        "v_out_w_scales": v_out_w_scales,
        "v_out_b": v_out_b,
        "mlp_w1_words": mlp_w1_words,
        "mlp_w1_scales": mlp_w1_scales,
        "mlp_b1": mlp_b1,
    }


def core(h_ctx, v_ctx, h_out_w_words, h_out_w_scales, h_out_b, v_out_w_words, v_out_w_scales, v_out_b, mlp_w1_words, mlp_w1_scales, mlp_b1):
    h_out = (mxq(f64(h_ctx), 2, "e4m3") @ unpack4(h_out_w_words, h_out_w_scales)) + f64(h_out_b)
    v_out = (mxq(f64(v_ctx), 2, "e4m3") @ unpack4(v_out_w_words, v_out_w_scales)) + f64(v_out_b)
    combined = np.concatenate([h_out, v_out], axis=-1)
    return np.maximum((mxq(combined, 2, "e4m3") @ unpack4(mlp_w1_words, mlp_w1_scales)) + f64(mlp_b1), 0.0)


def e4m3fn_bytes(y):
    return np.clip(np.asarray(y, np.float64), -448.0, 448.0).astype(np.float32).astype(ml_dtypes.float8_e4m3fn).view(np.uint8)


def e4m3fn_values(b):
    return np.asarray(b, np.uint8).view(ml_dtypes.float8_e4m3fn).astype(np.float64)


def setup_inputs():
    d = draw0()
    x0 = np.asarray(d['v_ctx']).astype(np.float64)
    s = (np.max(np.abs(x0), axis=(0, 1), keepdims=True) / 448.0).astype(np.float32)
    out = {}
    for k, v in d.items():
        if k == 'v_ctx':
            out['v_ctx_bytes'] = e4m3fn_bytes(x0 / s.astype(np.float64))
            out['v_ctx_scale'] = s
        else:
            out[k] = v
    return out


def reference(h_ctx, v_ctx_bytes, v_ctx_scale, h_out_w_words, h_out_w_scales, h_out_b, v_out_w_words, v_out_w_scales, v_out_b, mlp_w1_words, mlp_w1_scales, mlp_b1):
    return core(h_ctx, e4m3fn_values(v_ctx_bytes) * v_ctx_scale.astype(np.float64), h_out_w_words, h_out_w_scales, h_out_b, v_out_w_words, v_out_w_scales, v_out_b, mlp_w1_words, mlp_w1_scales, mlp_b1)

@@ -1,0 +1,260 @@
+from contextlib import ExitStack
+
+import concourse.mybir as mybir
+from concourse.masks import make_identity
+
+F32 = mybir.dt.float32
+BF16 = mybir.dt.bfloat16
+I32 = mybir.dt.int32
+U32 = mybir.dt.uint32
+U8 = mybir.dt.uint8
+FP8 = mybir.dt.float8_e4m3fn
+FP8X4 = mybir.dt.float8_e4m3fn_x4
+FP4X4 = mybir.dt.float4_e2m1fn_x4
+ADD = mybir.AluOpType.add
+MULT = mybir.AluOpType.mult
+RELU = mybir.ActivationFunctionType.Relu
+IDENT = mybir.ActivationFunctionType.Identity
+
+P = 128
+ROWS = 1024
+E = 512
+FLOPS = 2 * ROWS * E * E * 2 + 2 * ROWS * 2 * E * E
+GROUPS = 4
+
+
+def tile_bispa_pa_w4_kernel(
+    tc, h_ctx, v_bytes, v_scale, h_words, h_scales, h_b, v_words, v_scales, v_b, m_words, m_scales, m_b, out
+):
+    nc = tc.nc
+    h_rows = h_ctx.flatten_outer_dims().rearrange("(g p j) k -> g p j k", p=P, j=2)
+    v_rows = v_bytes.flatten_outer_dims().rearrange("(g p j) k -> g p j k", p=P, j=2)
+    o_rows = out.flatten_outer_dims().rearrange("(g p j) c -> g p j c", p=P, j=2)
+
+    with ExitStack() as ctx:
+        keep = ctx.enter_context(tc.tile_pool(name="keep", bufs=1))
+        work = ctx.enter_context(tc.tile_pool(name="work", bufs=3))
+        psum = ctx.enter_context(tc.psum_pool(name="psum", bufs=2))
+
+        ident = keep.tile([P, P], F32, name="ident")
+        ones_f = keep.tile([P, P], F32, name="ones_f")
+        ones_b = keep.tile([P, P], BF16, name="ones_b")
+        srow = keep.tile([P, E], F32, name="srow")
+        brow = keep.tile([P, E], BF16, name="brow")
+        scale_bc = keep.tile([P, E], F32, name="scale_bc")
+        bias_bc = keep.tile([P, E], F32, name="bias_bc")
+        raw_s = [keep.tile([P, E], U8, name=f"raw_s{i}", align_bytes=64) for i in range(2)]
+        perm_s = [keep.tile([P, E], U8, name=f"perm_s{i}", align_bytes=64) for i in range(2)]
+        raw_w = [keep.tile([P, 2 * E], U8, name=f"raw_w{i}", align_bytes=64) for i in range(2)]
+        perm_w = [keep.tile([P, 2 * E], U8, name=f"perm_w{i}", align_bytes=64) for i in range(2)]
+        bias1 = [keep.tile([P, 4], BF16, name=f"bias1_{i}") for i in range(2)]
+        mw = keep.tile([P, 2, 2 * E], U8, name="mw", align_bytes=64)
+        ms = keep.tile([P, 2, E], U8, name="ms", align_bytes=64)
+        h_in = [keep.tile([P, 2, E], BF16, name=f"h_in{g}", align_bytes=64) for g in range(GROUPS)]
+        v_in = [keep.tile([P, 2, E], U8, name=f"v_in{g}", align_bytes=64) for g in range(GROUPS)]
+
+        def load_scales(dst, src):
+            for r in range(4):
+                nc.sync.dma_start(
+                    out=dst[r:P:32, :].bitcast(I32),
+                    in_=src.rearrange("(q r) n -> r q n", r=4)[r].bitcast(I32),
+                )
+
+        ctx.enter_context(tc.manual_schedule())
+        nc.scalar.dma_start(out=h_in[0][:], in_=h_rows[0])
+        nc.sync.dma_start(out=raw_w[0][:].bitcast(I32), in_=h_words[0].bitcast(I32))
+        nc.vector.memset(raw_s[0][:].bitcast(I32), 0)
+        nc.vector.memset(srow[:], 0.0)
+        nc.vector.memset(raw_s[1][:].bitcast(I32), 0)
+        nc.vector.memset(brow[:], 0.0)
+        nc.vector.memset(ms[:].rearrange("p g n -> p (g n)").bitcast(I32), 0)
+        nc.gpsimd.memset(ones_f[:], 1.0)
+        nc.gpsimd.dma_start(out=srow[0:1, :], in_=v_scale.rearrange("a b k -> (a b) k"))
+        load_scales(raw_s[0], h_scales[0])
+        nc.sync.dma_start(out=raw_w[1][:].bitcast(I32), in_=v_words[0].bitcast(I32))
+        nc.sync.dma_start(out=v_in[0][:], in_=v_rows[0])
+        load_scales(raw_s[1], v_scales[0])
+        make_identity(nc, ident[:])
+        nc.gpsimd.memset(ones_b[:], 1.0)
+        nc.gpsimd.dma_start(out=bias1[0][:], in_=h_b.rearrange("(p t) -> p t", t=4))
+        nc.gpsimd.dma_start(out=bias1[1][:], in_=v_b.rearrange("(p t) -> p t", t=4))
+        nc.gpsimd.dma_start(out=brow[0:1, :], in_=m_b.rearrange("(o n) -> o n", o=1))
+        nc.sync.dma_start(out=h_in[1][:], in_=h_rows[1])
+        nc.sync.dma_start(out=v_in[1][:], in_=v_rows[1])
+        for g in range(2, GROUPS):
+            nc.sync.dma_start(out=h_in[g][:], in_=h_rows[g])
+            nc.sync.dma_start(out=v_in[g][:], in_=v_rows[g])
+        nc.sync.dma_start(
+            out=mw[:].bitcast(I32), in_=m_words.rearrange("g p n -> p g n").bitcast(I32)
+        )
+        for r in range(4):
+            nc.sync.dma_start(
+                out=ms[r:P:32, :, :].rearrange("p g n -> p (g n)").bitcast(I32).rearrange("p (g n) -> p g n", g=2),
+                in_=m_scales.rearrange("g (q r) n -> r q g n", r=4)[r].bitcast(I32),
+            )
+
+        def permute(i):
+            nc.vector.tensor_copy(
+                out=perm_w[i][:].rearrange("p (t m b) -> p t m b", t=4, b=2),
+                in_=raw_w[i][:].rearrange("p (m t b) -> p t m b", t=4, b=2),
+            )
+            nc.vector.tensor_copy(
+                out=perm_s[i][:].rearrange("p (t m) -> p t m", t=4),
+                in_=raw_s[i][:].rearrange("p (m t) -> p t m", t=4),
+            )
+
+        def spread_scale():
+            ps = psum.tile([P, E], F32, name="ops", bufs=2)
+            nc.tensor.matmul(ps[:], lhsT=ones_f[:], rhs=srow[:], start=True, stop=True)
+            nc.scalar.copy(out=scale_bc[:], in_=ps[:])
+
+        def spread_bias():
+            ps = psum.tile([P, E], F32, name="ops", bufs=2)
+            nc.tensor.matmul(ps[:], lhsT=ones_b[:], rhs=brow[:], start=True, stop=True)
+            nc.scalar.copy(out=bias_bc[:], in_=ps[:])
+
+        st = {}
+
+        def product(g):
+            prod = work.tile([P, 2, E], BF16, name="prod", align_bytes=64)
+            for j in range(2):
+                nc.vector.tensor_tensor(
+                    out=prod[:, j, :], in0=v_in[g][:, j, :].bitcast(FP8), in1=scale_bc[:], op=MULT
+                )
+            st["prod", g] = prod
+
+        def turn(g, i):
+            src = h_in[g] if i == 0 else st["prod", g]
+            words = src[:].rearrange("p j k -> p (j k)").bitcast(F32)
+            xt = psum.tile([P, 4, P], F32, name="xt", bufs=2)
+            for j in range(2):
+                for u in range(2):
+                    nc.tensor.transpose(xt[:, 2 * j + u, :], words[:, 256 * j + u : 256 * (j + 1) : 2], ident[:])
+            st["xt", g, i] = xt
+
+        def empty(g, i):
+            xg = work.tile([P, 2, P, 4], BF16, name="xg", align_bytes=64)
+            nc.scalar.copy(
+                out=xg[:].rearrange("p j n t -> p (j n t)").bitcast(F32).rearrange("p (j n u) -> p j n u", j=2, u=2),
+                in_=st["xt", g, i][:].rearrange("p (j u) n -> p j n u", u=2),
+            )
+            st["xg", g, i] = xg
+
+        def quant_x(g, i):
+            codes = work.tile([P, 2 * P], U32, name="xcodes", align_bytes=64)
+            scales = work.tile([P, 2 * P], U8, name="xscales", align_bytes=64)
+            nc.vector.quantize_mx(
+                out=codes[:].bitcast(FP8X4), scales=scales[:], in_=st["xg", g, i][:].rearrange("p j n t -> p (j n t)")
+            )
+            st["xq", g, i] = (codes, scales)
+
+        def project(g, i):
+            codes, scales = st["xq", g, i]
+            n = P if i == 0 else 2 * P
+            for half in range(2):
+                ps = psum.tile([P, E // n, n], F32, name="proj", bufs=4)
+                for q in range(E // n):
+                    t = q if i == 0 else 2 * half + q
+                    cols = slice(P * half, P * (half + 1)) if i == 0 else slice(0, 2 * P)
+                    nc.tensor.matmul_mx(
+                        out=ps[:, q, :],
+                        lhsT=perm_w[i][:, 2 * P * t : 2 * P * (t + 1)].bitcast(FP4X4),
+                        lhsT_scale=perm_s[i][:, P * t : P * (t + 1)],
+                        rhs=codes[:, cols].bitcast(FP8X4),
+                        rhs_scale=scales[:, cols],
+                        start=True,
+                        stop=True,
+                    )
+                st["proj", g, i, half] = ps
+
+        def combine_h(g):
+            comb = work.tile([P, 2 * P, 4], BF16, name="comb_h", align_bytes=64)
+            for j in range(2):
+                nc.vector.tensor_tensor(
+                    out=comb[:, P * j : P * (j + 1), :],
+                    in0=st["proj", g, 0, j][:].rearrange("p t n -> p n t"),
+                    in1=bias1[0][:].unsqueeze(1).to_broadcast([P, P, 4]),
+                    op=ADD,
+                )
+            st["comb", g, 0] = comb
+
+        def combine_v(g):
+            planes = work.tile([P, 4, 2 * P], BF16, name="planes", align_bytes=64)
+            for t in range(4):
+                nc.scalar.activation(
+                    out=planes[:, t, :],
+                    in_=st["proj", g, 1, t // 2][:, t % 2, :],
+                    func=IDENT,
+                    bias=bias1[1][:, t : t + 1],
+                )
+            comb = work.tile([P, 2 * P, 4], BF16, name="comb_v", align_bytes=64)
+            nc.scalar.copy(
+                out=comb[:].rearrange("p (c i) t -> p c t i", i=4),
+                in_=planes[:].rearrange("p t (c i) -> p c t i", i=4),
+            )
+            st["comb", g, 1] = comb
+
+        def quant_c(g, i):
+            codes = work.tile([P, 2 * P], U32, name="ccodes", bufs=4, align_bytes=64)
+            scales = work.tile([P, 2 * P], U8, name="cscales", bufs=4, align_bytes=64)
+            nc.vector.quantize_mx(
+                out=codes[:].bitcast(FP8X4), scales=scales[:], in_=st["comb", g, i][:].rearrange("p n t -> p (n t)")
+            )
+            st["cq", g, i] = (codes, scales)
+
+        def mix(g):
+            for j in range(2):
+                ps = psum.tile([P, E], F32, name="ops", bufs=2)
+                for i in range(2):
+                    codes, scales = st["cq", g, i]
+                    nc.tensor.matmul_mx(
+                        out=ps[:],
+                        lhsT=codes[:, P * j : P * (j + 1)].bitcast(FP8X4),
+                        lhsT_scale=scales[:, P * j : P * (j + 1)],
+                        rhs=mw[:, i, :].bitcast(FP4X4),
+                        rhs_scale=ms[:, i, :],
+                        start=(i == 0),
+                        stop=(i == 1),
+                    )
+                st["ops", g, j] = ps
+
+        def finish(g):
+            for j in range(2):
+                pre = work.tile([P, E], F32, name="pre", bufs=4)
+                nc.vector.tensor_tensor(out=pre[:], in0=st["ops", g, j][:], in1=bias_bc[:], op=ADD)
+                st["pre", g, j] = pre
+
+        def relu(g):
+            for j in range(2):
+                hid = work.tile([P, E], F32, name="hid", bufs=4)
+                nc.scalar.activation(out=hid[:], in_=st["pre", g, j][:], func=RELU)
+                nc.sync.dma_start(out=o_rows[g][:, j, :], in_=hid[:])
+
+        order = [
+            (lambda g: quant_x(g, 1), 1),
+            (lambda g: turn(g, 0), 2),
+            (lambda g: turn(g, 1), 2),
+            (lambda g: project(g, 1), 1),
+            (lambda g: quant_x(g, 0), 1),
+            (lambda g: project(g, 0), 1),
+            (lambda g: quant_c(g, 0), 0),
+            (lambda g: quant_c(g, 1), 0),
+            (product, 3),
+            (lambda g: empty(g, 0), 2),
+            (mix, 0),
+            (lambda g: empty(g, 1), 2),
+            (combine_h, 1),
+            (finish, 0),
+            (combine_v, 1),
+            (relu, 0),
+        ]
+        for step in range(-3, GROUPS):
+            if step == -3:
+                spread_scale()
+                permute(0)
+                permute(1)
+            if step == -2:
+                spread_bias()
+            for stage, ahead in order:
+                if 0 <= step + ahead < GROUPS:
+                    stage(step + ahead)

@@ -37,10 +37,9 @@ def tile_bispa_pa_w4_kernel(
         psum = ctx.enter_context(tc.psum_pool(name="psum", bufs=2))
 
         ident = keep.tile([P, P], F32, name="ident")
-        ones_f = keep.tile([P, P], F32, name="ones_f")
-        ones_b = keep.tile([P, P], BF16, name="ones_b")
-        srow = keep.tile([P, E], F32, name="srow")
-        brow = keep.tile([P, E], BF16, name="brow")
+        scale4 = keep.tile([P, 4], F32, name="scale4")
+        bias2 = keep.tile([P, 4], BF16, name="bias2")
+        bias2_f = keep.tile([P, 4], F32, name="bias2_f")
         scale_bc = keep.tile([P, E], F32, name="scale_bc")
         bias_bc = keep.tile([P, E], F32, name="bias_bc")
         raw_s = [keep.tile([P, E], U8, name=f"raw_s{i}", align_bytes=64) for i in range(2)]
@@ -61,37 +60,33 @@ def tile_bispa_pa_w4_kernel(
                 )
 
         ctx.enter_context(tc.manual_schedule())
-        nc.scalar.dma_start(out=h_in[0][:], in_=h_rows[0])
-        nc.sync.dma_start(out=raw_w[0][:].bitcast(I32), in_=h_words[0].bitcast(I32))
         nc.vector.memset(raw_s[0][:].bitcast(I32), 0)
-        nc.vector.memset(srow[:], 0.0)
         nc.vector.memset(raw_s[1][:].bitcast(I32), 0)
-        nc.vector.memset(brow[:], 0.0)
-        nc.vector.memset(ms[:].rearrange("p g n -> p (g n)").bitcast(I32), 0)
-        nc.gpsimd.memset(ones_f[:], 1.0)
-        nc.gpsimd.dma_start(out=srow[0:1, :], in_=v_scale.rearrange("a b k -> (a b) k"))
-        load_scales(raw_s[0], h_scales[0])
-        nc.sync.dma_start(out=raw_w[1][:].bitcast(I32), in_=v_words[0].bitcast(I32))
-        nc.sync.dma_start(out=v_in[0][:], in_=v_rows[0])
-        load_scales(raw_s[1], v_scales[0])
         make_identity(nc, ident[:])
-        nc.gpsimd.memset(ones_b[:], 1.0)
-        nc.gpsimd.dma_start(out=bias1[0][:], in_=h_b.rearrange("(p t) -> p t", t=4))
-        nc.gpsimd.dma_start(out=bias1[1][:], in_=v_b.rearrange("(p t) -> p t", t=4))
-        nc.gpsimd.dma_start(out=brow[0:1, :], in_=m_b.rearrange("(o n) -> o n", o=1))
-        nc.sync.dma_start(out=h_in[1][:], in_=h_rows[1])
+        nc.gpsimd.memset(ms[:].rearrange("p g n -> p (g n)").bitcast(I32), 0)
+        nc.scalar.dma_start(out=h_in[0][:], in_=h_rows[0])
+        nc.sync.dma_start(out=scale4[:], in_=v_scale.rearrange("a b (p t) -> p (a b t)", t=4))
+        nc.sync.dma_start(out=raw_w[0][:].bitcast(I32), in_=h_words[0].bitcast(I32))
+        load_scales(raw_s[0], h_scales[0])
+        nc.sync.dma_start(out=v_in[0][:], in_=v_rows[0])
         nc.sync.dma_start(out=v_in[1][:], in_=v_rows[1])
+        nc.sync.dma_start(out=h_in[1][:], in_=h_rows[1])
+        nc.sync.dma_start(out=raw_w[1][:].bitcast(I32), in_=v_words[0].bitcast(I32))
+        load_scales(raw_s[1], v_scales[0])
+        nc.gpsimd.dma_start(out=bias1[0][:], in_=h_b.rearrange("(p t) -> p t", t=4))
+        nc.gpsimd.dma_start(out=bias2[:], in_=m_b.rearrange("(p t) -> p t", t=4))
+        nc.gpsimd.dma_start(out=bias1[1][:], in_=v_b.rearrange("(p t) -> p t", t=4))
         for g in range(2, GROUPS):
             nc.sync.dma_start(out=h_in[g][:], in_=h_rows[g])
             nc.sync.dma_start(out=v_in[g][:], in_=v_rows[g])
-        nc.sync.dma_start(
-            out=mw[:].bitcast(I32), in_=m_words.rearrange("g p n -> p g n").bitcast(I32)
-        )
         for r in range(4):
             nc.sync.dma_start(
                 out=ms[r:P:32, :, :].rearrange("p g n -> p (g n)").bitcast(I32).rearrange("p (g n) -> p g n", g=2),
                 in_=m_scales.rearrange("g (q r) n -> r q g n", r=4)[r].bitcast(I32),
             )
+        nc.sync.dma_start(
+            out=mw[:].bitcast(I32), in_=m_words.rearrange("g p n -> p g n").bitcast(I32)
+        )
 
         def permute(i):
             nc.vector.tensor_copy(
@@ -103,15 +98,14 @@ def tile_bispa_pa_w4_kernel(
                 in_=raw_s[i][:].rearrange("p (m t) -> p t m", t=4),
             )
 
-        def spread_scale():
-            ps = psum.tile([P, E], F32, name="ops", bufs=2)
-            nc.tensor.matmul(ps[:], lhsT=ones_f[:], rhs=srow[:], start=True, stop=True)
-            nc.scalar.copy(out=scale_bc[:], in_=ps[:])
+        def spread(column4, name):
+            ps = psum.tile([P, 4, P], F32, name="ops", bufs=2)
+            for t in range(4):
+                nc.tensor.transpose(ps[:, t, :], column4[:, t : t + 1].to_broadcast([P, P]), ident[:])
+            return ps
 
-        def spread_bias():
-            ps = psum.tile([P, E], F32, name="ops", bufs=2)
-            nc.tensor.matmul(ps[:], lhsT=ones_b[:], rhs=brow[:], start=True, stop=True)
-            nc.scalar.copy(out=bias_bc[:], in_=ps[:])
+        def settle(ps, out):
+            nc.scalar.copy(out=out[:].rearrange("p (m t) -> p m t", t=4), in_=ps[:].rearrange("p t m -> p m t"))
 
         st = {}
 
@@ -227,34 +221,41 @@ def tile_bispa_pa_w4_kernel(
         def relu(g):
             for j in range(2):
                 hid = work.tile([P, E], F32, name="hid", bufs=4)
-                nc.scalar.activation(out=hid[:], in_=st["pre", g, j][:], func=RELU)
+                if (g, j) == (GROUPS - 1, 1):
+                    nc.vector.tensor_scalar(out=hid[:], in0=st["pre", g, j][:], scalar1=0.0, scalar2=None, op0=mybir.AluOpType.max)
+                else:
+                    nc.scalar.activation(out=hid[:], in_=st["pre", g, j][:], func=RELU)
                 nc.sync.dma_start(out=o_rows[g][:, j, :], in_=hid[:])
 
         order = [
             (lambda g: quant_x(g, 1), 1),
-            (lambda g: turn(g, 0), 2),
+            (lambda g: turn(g, 0), 3),
+            (lambda g: empty(g, 0), 3),
             (lambda g: turn(g, 1), 2),
-            (lambda g: project(g, 1), 1),
             (lambda g: quant_x(g, 0), 1),
-            (lambda g: project(g, 0), 1),
             (lambda g: quant_c(g, 0), 0),
-            (lambda g: quant_c(g, 1), 0),
-            (product, 3),
-            (lambda g: empty(g, 0), 2),
-            (mix, 0),
             (lambda g: empty(g, 1), 2),
-            (combine_h, 1),
-            (finish, 0),
+            (lambda g: project(g, 1), 1),
+            (lambda g: project(g, 0), 1),
+            (lambda g: quant_c(g, 1), 0),
             (combine_v, 1),
+            (product, 3),
+            (combine_h, 1),
+            (mix, 0),
+            (finish, 0),
             (relu, 0),
         ]
         for step in range(-3, GROUPS):
             if step == -3:
-                spread_scale()
+                sp = spread(scale4, "sp")
                 permute(0)
-                permute(1)
+                settle(sp, scale_bc)
             if step == -2:
-                spread_bias()
+                nc.vector.tensor_copy(out=bias2_f[:], in_=bias2[:])
+                bp = spread(bias2_f, "bp")
+            if step == -1:
+                permute(1)
+                settle(bp, bias_bc)
             for stage, ahead in order:
                 if 0 <= step + ahead < GROUPS:
                     stage(step + ahead)

from contextlib import ExitStack

import concourse.mybir as mybir
from concourse.masks import make_identity

F32 = mybir.dt.float32
BF16 = mybir.dt.bfloat16
I32 = mybir.dt.int32
U32 = mybir.dt.uint32
U8 = mybir.dt.uint8
FP8 = mybir.dt.float8_e4m3fn
FP8X4 = mybir.dt.float8_e4m3fn_x4
FP4X4 = mybir.dt.float4_e2m1fn_x4
ADD = mybir.AluOpType.add
MULT = mybir.AluOpType.mult
RELU = mybir.ActivationFunctionType.Relu
IDENT = mybir.ActivationFunctionType.Identity

P = 128
ROWS = 1024
E = 512
FLOPS = 2 * ROWS * E * E * 2 + 2 * ROWS * 2 * E * E
GROUPS = 4


def tile_bispa_pa_w4_kernel(
    tc, h_ctx, v_bytes, v_scale, h_words, h_scales, h_b, v_words, v_scales, v_b, m_words, m_scales, m_b, out
):
    nc = tc.nc
    h_rows = h_ctx.flatten_outer_dims().rearrange("(g p j) k -> g p j k", p=P, j=2)
    v_rows = v_bytes.flatten_outer_dims().rearrange("(g p j) k -> g p j k", p=P, j=2)
    o_rows = out.flatten_outer_dims().rearrange("(g p j) c -> g p j c", p=P, j=2)

    with ExitStack() as ctx:
        keep = ctx.enter_context(tc.tile_pool(name="keep", bufs=1))
        work = ctx.enter_context(tc.tile_pool(name="work", bufs=3))
        psum = ctx.enter_context(tc.psum_pool(name="psum", bufs=2))

        ident = keep.tile([P, P], F32, name="ident")
        scale4 = keep.tile([P, 4], F32, name="scale4")
        bias2 = keep.tile([P, 4], BF16, name="bias2")
        bias2_f = keep.tile([P, 4], F32, name="bias2_f")
        scale_bc = keep.tile([P, E], F32, name="scale_bc")
        bias_bc = keep.tile([P, E], F32, name="bias_bc")
        raw_s = [keep.tile([P, E], U8, name=f"raw_s{i}", align_bytes=64) for i in range(2)]
        perm_s = [keep.tile([P, E], U8, name=f"perm_s{i}", align_bytes=64) for i in range(2)]
        raw_w = [keep.tile([P, 2 * E], U8, name=f"raw_w{i}", align_bytes=64) for i in range(2)]
        perm_w = [keep.tile([P, 2 * E], U8, name=f"perm_w{i}", align_bytes=64) for i in range(2)]
        bias1 = [keep.tile([P, 4], BF16, name=f"bias1_{i}") for i in range(2)]
        mw = keep.tile([P, 2, 2 * E], U8, name="mw", align_bytes=64)
        ms = keep.tile([P, 2, E], U8, name="ms", align_bytes=64)
        h_in = [keep.tile([P, 2, E], BF16, name=f"h_in{g}", align_bytes=64) for g in range(GROUPS)]
        v_in = [keep.tile([P, 2, E], U8, name=f"v_in{g}", align_bytes=64) for g in range(GROUPS)]

        def load_scales(dst, src):
            for r in range(4):
                nc.sync.dma_start(
                    out=dst[r:P:32, :].bitcast(I32),
                    in_=src.rearrange("(q r) n -> r q n", r=4)[r].bitcast(I32),
                )

        ctx.enter_context(tc.manual_schedule())
        nc.vector.memset(raw_s[0][:].bitcast(I32), 0)
        nc.vector.memset(raw_s[1][:].bitcast(I32), 0)
        make_identity(nc, ident[:])
        nc.gpsimd.memset(ms[:].rearrange("p g n -> p (g n)").bitcast(I32), 0)
        nc.scalar.dma_start(out=h_in[0][:], in_=h_rows[0])
        nc.sync.dma_start(out=scale4[:], in_=v_scale.rearrange("a b (p t) -> p (a b t)", t=4))
        nc.sync.dma_start(out=raw_w[0][:].bitcast(I32), in_=h_words[0].bitcast(I32))
        load_scales(raw_s[0], h_scales[0])
        nc.sync.dma_start(out=v_in[0][:], in_=v_rows[0])
        nc.sync.dma_start(out=v_in[1][:], in_=v_rows[1])
        nc.sync.dma_start(out=h_in[1][:], in_=h_rows[1])
        nc.sync.dma_start(out=raw_w[1][:].bitcast(I32), in_=v_words[0].bitcast(I32))
        load_scales(raw_s[1], v_scales[0])
        nc.gpsimd.dma_start(out=bias1[0][:], in_=h_b.rearrange("(p t) -> p t", t=4))
        nc.gpsimd.dma_start(out=bias2[:], in_=m_b.rearrange("(p t) -> p t", t=4))
        nc.gpsimd.dma_start(out=bias1[1][:], in_=v_b.rearrange("(p t) -> p t", t=4))
        for g in range(2, GROUPS):
            nc.sync.dma_start(out=h_in[g][:], in_=h_rows[g])
            nc.sync.dma_start(out=v_in[g][:], in_=v_rows[g])
        for r in range(4):
            nc.sync.dma_start(
                out=ms[r:P:32, :, :].rearrange("p g n -> p (g n)").bitcast(I32).rearrange("p (g n) -> p g n", g=2),
                in_=m_scales.rearrange("g (q r) n -> r q g n", r=4)[r].bitcast(I32),
            )
        nc.sync.dma_start(
            out=mw[:].bitcast(I32), in_=m_words.rearrange("g p n -> p g n").bitcast(I32)
        )

        def permute(i):
            nc.vector.tensor_copy(
                out=perm_w[i][:].rearrange("p (t m b) -> p t m b", t=4, b=2),
                in_=raw_w[i][:].rearrange("p (m t b) -> p t m b", t=4, b=2),
            )
            nc.vector.tensor_copy(
                out=perm_s[i][:].rearrange("p (t m) -> p t m", t=4),
                in_=raw_s[i][:].rearrange("p (m t) -> p t m", t=4),
            )

        def spread(column4, name):
            ps = psum.tile([P, 4, P], F32, name="ops", bufs=2)
            for t in range(4):
                nc.tensor.transpose(ps[:, t, :], column4[:, t : t + 1].to_broadcast([P, P]), ident[:])
            return ps

        def settle(ps, out):
            nc.scalar.copy(out=out[:].rearrange("p (m t) -> p m t", t=4), in_=ps[:].rearrange("p t m -> p m t"))

        st = {}

        def product(g):
            prod = work.tile([P, 2, E], BF16, name="prod", align_bytes=64)
            for j in range(2):
                nc.vector.tensor_tensor(
                    out=prod[:, j, :], in0=v_in[g][:, j, :].bitcast(FP8), in1=scale_bc[:], op=MULT
                )
            st["prod", g] = prod

        def turn(g, i):
            src = h_in[g] if i == 0 else st["prod", g]
            words = src[:].rearrange("p j k -> p (j k)").bitcast(F32)
            xt = psum.tile([P, 4, P], F32, name="xt", bufs=2)
            for j in range(2):
                for u in range(2):
                    nc.tensor.transpose(xt[:, 2 * j + u, :], words[:, 256 * j + u : 256 * (j + 1) : 2], ident[:])
            st["xt", g, i] = xt

        def empty(g, i):
            xg = work.tile([P, 2, P, 4], BF16, name="xg", align_bytes=64)
            nc.scalar.copy(
                out=xg[:].rearrange("p j n t -> p (j n t)").bitcast(F32).rearrange("p (j n u) -> p j n u", j=2, u=2),
                in_=st["xt", g, i][:].rearrange("p (j u) n -> p j n u", u=2),
            )
            st["xg", g, i] = xg

        def quant_x(g, i):
            codes = work.tile([P, 2 * P], U32, name="xcodes", align_bytes=64)
            scales = work.tile([P, 2 * P], U8, name="xscales", align_bytes=64)
            nc.vector.quantize_mx(
                out=codes[:].bitcast(FP8X4), scales=scales[:], in_=st["xg", g, i][:].rearrange("p j n t -> p (j n t)")
            )
            st["xq", g, i] = (codes, scales)

        def project(g, i):
            codes, scales = st["xq", g, i]
            n = P if i == 0 else 2 * P
            for half in range(2):
                ps = psum.tile([P, E // n, n], F32, name="proj", bufs=4)
                for q in range(E // n):
                    t = q if i == 0 else 2 * half + q
                    cols = slice(P * half, P * (half + 1)) if i == 0 else slice(0, 2 * P)
                    nc.tensor.matmul_mx(
                        out=ps[:, q, :],
                        lhsT=perm_w[i][:, 2 * P * t : 2 * P * (t + 1)].bitcast(FP4X4),
                        lhsT_scale=perm_s[i][:, P * t : P * (t + 1)],
                        rhs=codes[:, cols].bitcast(FP8X4),
                        rhs_scale=scales[:, cols],
                        start=True,
                        stop=True,
                    )
                st["proj", g, i, half] = ps

        def combine_h(g):
            comb = work.tile([P, 2 * P, 4], BF16, name="comb_h", align_bytes=64)
            for j in range(2):
                nc.vector.tensor_tensor(
                    out=comb[:, P * j : P * (j + 1), :],
                    in0=st["proj", g, 0, j][:].rearrange("p t n -> p n t"),
                    in1=bias1[0][:].unsqueeze(1).to_broadcast([P, P, 4]),
                    op=ADD,
                )
            st["comb", g, 0] = comb

        def combine_v(g):
            planes = work.tile([P, 4, 2 * P], BF16, name="planes", align_bytes=64)
            for t in range(4):
                nc.scalar.activation(
                    out=planes[:, t, :],
                    in_=st["proj", g, 1, t // 2][:, t % 2, :],
                    func=IDENT,
                    bias=bias1[1][:, t : t + 1],
                )
            comb = work.tile([P, 2 * P, 4], BF16, name="comb_v", align_bytes=64)
            nc.scalar.copy(
                out=comb[:].rearrange("p (c i) t -> p c t i", i=4),
                in_=planes[:].rearrange("p t (c i) -> p c t i", i=4),
            )
            st["comb", g, 1] = comb

        def quant_c(g, i):
            codes = work.tile([P, 2 * P], U32, name="ccodes", bufs=4, align_bytes=64)
            scales = work.tile([P, 2 * P], U8, name="cscales", bufs=4, align_bytes=64)
            nc.vector.quantize_mx(
                out=codes[:].bitcast(FP8X4), scales=scales[:], in_=st["comb", g, i][:].rearrange("p n t -> p (n t)")
            )
            st["cq", g, i] = (codes, scales)

        def mix(g):
            for j in range(2):
                ps = psum.tile([P, E], F32, name="ops", bufs=2)
                for i in range(2):
                    codes, scales = st["cq", g, i]
                    nc.tensor.matmul_mx(
                        out=ps[:],
                        lhsT=codes[:, P * j : P * (j + 1)].bitcast(FP8X4),
                        lhsT_scale=scales[:, P * j : P * (j + 1)],
                        rhs=mw[:, i, :].bitcast(FP4X4),
                        rhs_scale=ms[:, i, :],
                        start=(i == 0),
                        stop=(i == 1),
                    )
                st["ops", g, j] = ps

        def finish(g):
            for j in range(2):
                pre = work.tile([P, E], F32, name="pre", bufs=4)
                nc.vector.tensor_tensor(out=pre[:], in0=st["ops", g, j][:], in1=bias_bc[:], op=ADD)
                st["pre", g, j] = pre

        def relu(g):
            for j in range(2):
                hid = work.tile([P, E], F32, name="hid", bufs=4)
                if (g, j) == (GROUPS - 1, 1):
                    nc.vector.tensor_scalar(out=hid[:], in0=st["pre", g, j][:], scalar1=0.0, scalar2=None, op0=mybir.AluOpType.max)
                else:
                    nc.scalar.activation(out=hid[:], in_=st["pre", g, j][:], func=RELU)
                nc.sync.dma_start(out=o_rows[g][:, j, :], in_=hid[:])

        order = [
            (lambda g: quant_x(g, 1), 1),
            (lambda g: turn(g, 0), 3),
            (lambda g: empty(g, 0), 3),
            (lambda g: turn(g, 1), 2),
            (lambda g: quant_x(g, 0), 1),
            (lambda g: quant_c(g, 0), 0),
            (lambda g: empty(g, 1), 2),
            (lambda g: project(g, 1), 1),
            (lambda g: project(g, 0), 1),
            (lambda g: quant_c(g, 1), 0),
            (combine_v, 1),
            (product, 3),
            (combine_h, 1),
            (mix, 0),
            (finish, 0),
            (relu, 0),
        ]
        for step in range(-3, GROUPS):
            if step == -3:
                sp = spread(scale4, "sp")
                permute(0)
                settle(sp, scale_bc)
            if step == -2:
                nc.vector.tensor_copy(out=bias2_f[:], in_=bias2[:])
                bp = spread(bias2_f, "bp")
            if step == -1:
                permute(1)
                settle(bp, bias_bc)
            for stage, ahead in order:
                if 0 <= step + ahead < GROUPS:
                    stage(step + ahead)
